import numpy as np
import ml_dtypes


def mxq(x, axis, fmt="e4m3"):
    dtype, down = {"e4m3": (ml_dtypes.float8_e4m3fn, 7), "e5m2": (ml_dtypes.float8_e5m2, 14)}[fmt]
    v = np.moveaxis(np.asarray(x, np.float32).astype(ml_dtypes.bfloat16).astype(np.float64), axis, -1)
    blocks = v.reshape(v.shape[:-1] + (-1, 32))
    amax = np.abs(blocks).max(-1, keepdims=True)
    byte = np.maximum(np.where(amax > 0, np.frexp(amax)[1] - 1 + 127, 0) - down, 1)
    scale = np.exp2(byte - 127.0)
    codes = (blocks / scale).astype(np.float32).astype(dtype).astype(np.float64)
    return np.moveaxis((codes * scale).reshape(v.shape), -1, axis)


WIDE = False


def mx_kscale(k):
    if not WIDE:
        return np.ones(k)
    levels = np.array([10, -10, 5, -5, 0])
    a = np.random.permutation(np.resize(levels, k // 512 * 4)).reshape(k // 512, 4)
    idx = np.arange(k)
    return np.exp2(a[idx // 512, idx % 128 // 32])


BF16 = ml_dtypes.bfloat16


def bf(x):
    return np.asarray(x, np.float32).astype(BF16)


def f64(x):
    return np.asarray(x).astype(np.float64)


E2M1 = np.array([0.0, 0.5, 1.0, 1.5, 2.0, 3.0, 4.0, 6.0, -0.0, -0.5, -1.0, -1.5, -2.0, -3.0, -4.0, -6.0])


def pack_weight(w, fmt):
    k, n = w.shape
    w = f64(bf(w)).reshape(k // 32, 32, n)
    amax = np.abs(w).max(1)
    if fmt == "e4m3":
        byte = np.frexp(amax)[1] - 1 + 127 - 7
    else:
        mant, ex = np.frexp(amax / 6.0)
        byte = np.where(mant > 0.5, ex, ex - 1) + 127
    byte = np.clip(np.where(amax > 0, byte, 1), 1, 254)
    scaled = (w * np.exp2(127.0 - byte)[:, None, :]).reshape(k, n).astype(np.float32)
    by_word = np.ascontiguousarray(scaled.reshape(k // 512, 128, 4, n).transpose(0, 1, 3, 2))
    if fmt == "e4m3":
        words = by_word.astype(ml_dtypes.float8_e4m3fn).view(np.uint8)
    else:
        c = by_word.astype(ml_dtypes.float4_e2m1fn).view(np.uint8) & 0xF
        words = c[..., 0::2] | (c[..., 1::2] << 4)
    return np.ascontiguousarray(words), np.ascontiguousarray(byte.astype(np.uint8).reshape(k // 512, 16, n))


def unpack_weight(words, scales, fmt):
    g, p, n, _ = words.shape
    if fmt == "e4m3":
        vals = np.ascontiguousarray(words).view(ml_dtypes.float8_e4m3fn).astype(np.float64)
    else:
        nib = np.empty((g, p, n, 4), np.uint8)
        nib[..., 0::2] = words & 0xF
        nib[..., 1::2] = words >> 4
        vals = E2M1[nib]
    vals = vals * np.repeat(np.exp2(scales.astype(np.float64) - 127.0), 8, axis=1)[..., None]
    return vals.transpose(0, 1, 3, 2).reshape(g * 512, n)


B, D, K = 640, 512, 4


def setup_inputs():
    s = mx_kscale(D)
    x = np.random.standard_normal((B, D, K)) * s[None, :, None]
    mu = np.random.standard_normal((D, K)) * 0.3 * s[:, None]
    w = (np.eye(D)[None] + np.random.standard_normal((K, D, D)) * 0.7 / np.sqrt(D)) / s[None, None, :]
    cat = np.ascontiguousarray(w.swapaxes(1, 2)).reshape(-1, D)
    words, scales = pack_weight(cat, "e4m3")
    return {"x": bf(x), "mu_track": bf(mu), "Std_inv_track_words": words, "Std_inv_track_scales": scales}


def reference(x, mu_track, Std_inv_track_words, Std_inv_track_scales):
    x_cnt = f64(x) - f64(mu_track)[None]
    xq = mxq(x_cnt, 1, "e4m3")
    wq = unpack_weight(Std_inv_track_words, Std_inv_track_scales, "e4m3").reshape(K, D, D).swapaxes(1, 2)
    z = wq @ xq.transpose(2, 1, 0)
    return z.transpose(2, 1, 0)

@@ -1,0 +1,156 @@
+from contextlib import ExitStack
+
+import concourse.mybir as mybir
+from concourse.masks import make_identity
+
+F32 = mybir.dt.float32
+BF16 = mybir.dt.bfloat16
+I32 = mybir.dt.int32
+U32 = mybir.dt.uint32
+U8 = mybir.dt.uint8
+FP8X4 = mybir.dt.float8_e4m3fn_x4
+
+P = 128
+PACK = 4
+BATCH, FEATURES, CLUSTERS = 640, 512, 4
+PAIRS = CLUSTERS // 2
+BATCH_TILES = BATCH // P
+HALVES = BATCH_TILES * PAIRS
+D_TILE = 128
+D_TILES = FEATURES // D_TILE
+ROW = FEATURES * CLUSTERS
+WORDS_PER_P = ROW // 2 // P
+QUADRANTS = 4
+
+FLOPS = 2 * BATCH * FEATURES * FEATURES * CLUSTERS
+
+
+def tile_clusternorm1dv3_e_kernel(tc, x, mu_track, w_words, w_scales, out):
+    nc = tc.nc
+    x_rows = x.rearrange("(n b) e k -> n b (e k)", b=P)
+    out_rows = out.rearrange("(n b) d k -> n b (d k)", b=P)
+
+    with ExitStack() as ctx:
+        keep = ctx.enter_context(tc.tile_pool(name="keep", bufs=1))
+        centred_pool = ctx.enter_context(tc.tile_pool(name="centred_pool", bufs=3))
+        result_pool = ctx.enter_context(tc.tile_pool(name="result_pool", bufs=8))
+        xt_pool = ctx.enter_context(tc.psum_pool(name="xt_pool", bufs=2 * PAIRS))
+        product_pool = ctx.enter_context(tc.psum_pool(name="product_pool", bufs=D_TILES))
+        ctx.enter_context(tc.manual_schedule())
+
+        identity = keep.tile([P, P], F32)
+        mu_sb = keep.tile([P, PACK * CLUSTERS], BF16)
+        w_codes = keep.tile([P, CLUSTERS, FEATURES], U32, align_bytes=64)
+        w_planes = keep.tile([P, FEATURES], U8, align_bytes=64)
+        x_sb = [keep.tile([P, ROW], BF16, name="x_sb%d" % n) for n in range(BATCH_TILES)]
+        x_codes = [
+            keep.tile([P, CLUSTERS, P], U32, name="x_codes%d" % n, align_bytes=64)
+            for n in range(BATCH_TILES)
+        ]
+        x_planes = [
+            keep.tile([P, CLUSTERS, P], U8, name="x_planes%d" % n, align_bytes=64)
+            for n in range(BATCH_TILES)
+        ]
+
+        nc.vector.memset(w_planes[:].bitcast(I32), 0)
+        make_identity(nc, identity[:])
+
+        def load_x(n):
+            nc.sync.dma_start(out=x_sb[n][:], in_=x_rows[n])
+
+        nc.sync.dma_start(out=mu_sb[:], in_=mu_track.rearrange("(p t) k -> p (t k)", t=PACK))
+        load_x(0)
+        load_x(1)
+        load_x(2)
+        for quadrant in range(QUADRANTS):
+            nc.sync.dma_start(
+                out=w_planes[32 * quadrant : 32 * quadrant + 4 * CLUSTERS, :].bitcast(I32),
+                in_=w_scales[:, 4 * quadrant : 4 * quadrant + 4, :].bitcast(I32),
+            )
+        nc.sync.dma_start(
+            out=w_codes[:].bitcast(I32),
+            in_=w_words.rearrange("k p d t -> p k (d t)").bitcast(I32),
+        )
+        load_x(3)
+        load_x(4)
+
+        xt_banks = {}
+        centred_tiles = {}
+        product_banks = {}
+
+        def transpose_tile(n):
+            words = x_sb[n][:].bitcast(F32)
+            for pair in range(PAIRS):
+                xt = xt_pool.tile([P, PACK, P], F32, name="xt")
+                for t in range(PACK):
+                    nc.tensor.transpose(
+                        xt[:, t, :],
+                        words[:, PAIRS * t + pair : ROW // 2 : WORDS_PER_P],
+                        identity[:],
+                    )
+                xt_banks[PAIRS * n + pair] = xt
+
+        def centre(half):
+            pair = half % PAIRS
+            centred = centred_pool.tile([P, 2, P, PACK], BF16, name="centred", align_bytes=64)
+            mu_of_pair = mu_sb[:].rearrange("p (t k) -> p k t", k=CLUSTERS)[:, 2 * pair : 2 * pair + 2, :]
+            nc.vector.tensor_tensor(
+                out=centred[:],
+                in0=xt_banks[half][:].bitcast(BF16).rearrange("p t (b c) -> p c b t", c=2),
+                in1=mu_of_pair.unsqueeze(2).to_broadcast([P, 2, P, PACK]),
+                op=mybir.AluOpType.subtract,
+            )
+            centred_tiles[half] = centred
+
+        def quantise(half):
+            n, pair = divmod(half, PAIRS)
+            clusters = slice(2 * pair, 2 * pair + 2)
+            nc.vector.quantize_mx(
+                out=x_codes[n][:, clusters, :].rearrange("p c b -> p (c b)").bitcast(FP8X4),
+                scales=x_planes[n][:, clusters, :].rearrange("p c b -> p (c b)"),
+                in_=centred_tiles[half][:].rearrange("p c b t -> p (c b t)"),
+            )
+
+        def multiply(half):
+            n, pair = divmod(half, PAIRS)
+            for j in range(D_TILES):
+                if pair == 0:
+                    product_banks[(n, j)] = product_pool.tile([P, CLUSTERS, D_TILE], F32, name="product")
+                d_cols = slice(D_TILE * j, D_TILE * (j + 1))
+                for k in range(2 * pair, 2 * pair + 2):
+                    nc.tensor.matmul_mx(
+                        out=product_banks[(n, j)][:, k, :],
+                        lhsT=x_codes[n][:, k, :].bitcast(FP8X4),
+                        lhsT_scale=x_planes[n][:, k, :],
+                        rhs=w_codes[:, k, d_cols].bitcast(FP8X4),
+                        rhs_scale=w_planes[4 * k : P, d_cols],
+                        start=True,
+                        stop=True,
+                    )
+
+        def copy_out_and_store(n):
+            for j in range(D_TILES):
+                result = result_pool.tile([P, D_TILE, CLUSTERS], F32, name="result")
+                interleaved = product_banks[(n, j)][:].rearrange("b k d -> b d k")
+                if n == BATCH_TILES - 1 and j % 2 == 1:
+                    nc.vector.tensor_copy(out=result[:], in_=interleaved)
+                else:
+                    nc.scalar.copy(out=result[:], in_=interleaved)
+                nc.sync.dma_start(
+                    out=out_rows[n][:, D_TILE * CLUSTERS * j : D_TILE * CLUSTERS * (j + 1)],
+                    in_=result[:].rearrange("b d k -> b (d k)"),
+                )
+
+        transpose_tile(0)
+        transpose_tile(1)
+        for i in range(HALVES + 1):
+            if i < HALVES:
+                centre(i)
+            if i >= 1:
+                quantise(i - 1)
+            if i < HALVES and i % PAIRS == PAIRS - 1 and i // PAIRS + 2 < BATCH_TILES:
+                transpose_tile(i // PAIRS + 2)
+            if i >= 1:
+                multiply(i - 1)
+                if (i - 1) % PAIRS == PAIRS - 1:
+                    copy_out_and_store((i - 1) // PAIRS)

@@ -15,12 +15,12 @@ PACK = 4
 BATCH, FEATURES, CLUSTERS = 640, 512, 4
 PAIRS = CLUSTERS // 2
 BATCH_TILES = BATCH // P
-HALVES = BATCH_TILES * PAIRS
 D_TILE = 128
 D_TILES = FEATURES // D_TILE
 ROW = FEATURES * CLUSTERS
 WORDS_PER_P = ROW // 2 // P
 QUADRANTS = 4
+SCALAR_HELPS_TILES = 2
 
 FLOPS = 2 * BATCH * FEATURES * FEATURES * CLUSTERS
 
@@ -32,7 +32,8 @@ def tile_clusternorm1dv3_e_kernel(tc, x, mu_track, w_words, w_scales, out):
 
     with ExitStack() as ctx:
         keep = ctx.enter_context(tc.tile_pool(name="keep", bufs=1))
-        centred_pool = ctx.enter_context(tc.tile_pool(name="centred_pool", bufs=3))
+        ordered_pool = ctx.enter_context(tc.tile_pool(name="ordered_pool", bufs=2))
+        centred_pool = ctx.enter_context(tc.tile_pool(name="centred_pool", bufs=4))
         result_pool = ctx.enter_context(tc.tile_pool(name="result_pool", bufs=8))
         xt_pool = ctx.enter_context(tc.psum_pool(name="xt_pool", bufs=2 * PAIRS))
         product_pool = ctx.enter_context(tc.psum_pool(name="product_pool", bufs=D_TILES))
@@ -61,7 +62,6 @@ def tile_clusternorm1dv3_e_kernel(tc, x, mu_track, w_words, w_scales, out):
         nc.sync.dma_start(out=mu_sb[:], in_=mu_track.rearrange("(p t) k -> p (t k)", t=PACK))
         load_x(0)
         load_x(1)
-        load_x(2)
         for quadrant in range(QUADRANTS):
             nc.sync.dma_start(
                 out=w_planes[32 * quadrant : 32 * quadrant + 4 * CLUSTERS, :].bitcast(I32),
@@ -71,6 +71,7 @@ def tile_clusternorm1dv3_e_kernel(tc, x, mu_track, w_words, w_scales, out):
             out=w_codes[:].bitcast(I32),
             in_=w_words.rearrange("k p d t -> p k (d t)").bitcast(I32),
         )
+        load_x(2)
         load_x(3)
         load_x(4)
 
@@ -91,12 +92,17 @@ def tile_clusternorm1dv3_e_kernel(tc, x, mu_track, w_words, w_scales, out):
                 xt_banks[PAIRS * n + pair] = xt
 
         def centre(half):
-            pair = half % PAIRS
+            n, pair = divmod(half, PAIRS)
             centred = centred_pool.tile([P, 2, P, PACK], BF16, name="centred", align_bytes=64)
+            in_order = xt_banks[half][:].bitcast(BF16).rearrange("p t (b c) -> p c b t", c=2)
+            if pair == PAIRS - 1 and n < SCALAR_HELPS_TILES:
+                ordered = ordered_pool.tile([P, 2, P, PACK], BF16, name="ordered")
+                nc.scalar.copy(out=ordered[:], in_=in_order)
+                in_order = ordered[:]
             mu_of_pair = mu_sb[:].rearrange("p (t k) -> p k t", k=CLUSTERS)[:, 2 * pair : 2 * pair + 2, :]
             nc.vector.tensor_tensor(
                 out=centred[:],
-                in0=xt_banks[half][:].bitcast(BF16).rearrange("p t (b c) -> p c b t", c=2),
+                in0=in_order,
                 in1=mu_of_pair.unsqueeze(2).to_broadcast([P, 2, P, PACK]),
                 op=mybir.AluOpType.subtract,
             )
@@ -111,15 +117,19 @@ def tile_clusternorm1dv3_e_kernel(tc, x, mu_track, w_words, w_scales, out):
                 in_=centred_tiles[half][:].rearrange("p c b t -> p (c b t)"),
             )
 
-        def multiply(half):
-            n, pair = divmod(half, PAIRS)
+        def prepare_tile(n):
+            for pair in range(PAIRS):
+                centre(PAIRS * n + pair)
+            for pair in range(PAIRS):
+                quantise(PAIRS * n + pair)
+
+        def multiply_tile(n):
             for j in range(D_TILES):
-                if pair == 0:
-                    product_banks[(n, j)] = product_pool.tile([P, CLUSTERS, D_TILE], F32, name="product")
+                product = product_pool.tile([P, CLUSTERS, D_TILE], F32, name="product")
                 d_cols = slice(D_TILE * j, D_TILE * (j + 1))
-                for k in range(2 * pair, 2 * pair + 2):
+                for k in range(CLUSTERS):
                     nc.tensor.matmul_mx(
-                        out=product_banks[(n, j)][:, k, :],
+                        out=product[:, k, :],
                         lhsT=x_codes[n][:, k, :].bitcast(FP8X4),
                         lhsT_scale=x_planes[n][:, k, :],
                         rhs=w_codes[:, k, d_cols].bitcast(FP8X4),
@@ -127,6 +137,7 @@ def tile_clusternorm1dv3_e_kernel(tc, x, mu_track, w_words, w_scales, out):
                         start=True,
                         stop=True,
                     )
+                product_banks[(n, j)] = product
 
         def copy_out_and_store(n):
             for j in range(D_TILES):
@@ -143,14 +154,11 @@ def tile_clusternorm1dv3_e_kernel(tc, x, mu_track, w_words, w_scales, out):
 
         transpose_tile(0)
         transpose_tile(1)
-        for i in range(HALVES + 1):
-            if i < HALVES:
-                centre(i)
-            if i >= 1:
-                quantise(i - 1)
-            if i < HALVES and i % PAIRS == PAIRS - 1 and i // PAIRS + 2 < BATCH_TILES:
-                transpose_tile(i // PAIRS + 2)
-            if i >= 1:
-                multiply(i - 1)
-                if (i - 1) % PAIRS == PAIRS - 1:
-                    copy_out_and_store((i - 1) // PAIRS)
+        prepare_tile(0)
+        for n in range(BATCH_TILES):
+            multiply_tile(n)
+            if n + 2 < BATCH_TILES:
+                transpose_tile(n + 2)
+            if n + 1 < BATCH_TILES:
+                prepare_tile(n + 1)
+            copy_out_and_store(n)

@@ -20,7 +20,7 @@ D_TILES = FEATURES // D_TILE
 ROW = FEATURES * CLUSTERS
 WORDS_PER_P = ROW // 2 // P
 QUADRANTS = 4
-SCALAR_HELPS_TILES = 2
+SCALAR_HELPS_TILE = 1
 
 FLOPS = 2 * BATCH * FEATURES * FEATURES * CLUSTERS
 
@@ -32,7 +32,7 @@ def tile_clusternorm1dv3_e_kernel(tc, x, mu_track, w_words, w_scales, out):
 
     with ExitStack() as ctx:
         keep = ctx.enter_context(tc.tile_pool(name="keep", bufs=1))
-        ordered_pool = ctx.enter_context(tc.tile_pool(name="ordered_pool", bufs=2))
+        ordered_pool = ctx.enter_context(tc.tile_pool(name="ordered_pool", bufs=1))
         centred_pool = ctx.enter_context(tc.tile_pool(name="centred_pool", bufs=4))
         result_pool = ctx.enter_context(tc.tile_pool(name="result_pool", bufs=8))
         xt_pool = ctx.enter_context(tc.psum_pool(name="xt_pool", bufs=2 * PAIRS))
@@ -62,6 +62,7 @@ def tile_clusternorm1dv3_e_kernel(tc, x, mu_track, w_words, w_scales, out):
         nc.sync.dma_start(out=mu_sb[:], in_=mu_track.rearrange("(p t) k -> p (t k)", t=PACK))
         load_x(0)
         load_x(1)
+        load_x(2)
         for quadrant in range(QUADRANTS):
             nc.sync.dma_start(
                 out=w_planes[32 * quadrant : 32 * quadrant + 4 * CLUSTERS, :].bitcast(I32),
@@ -71,7 +72,6 @@ def tile_clusternorm1dv3_e_kernel(tc, x, mu_track, w_words, w_scales, out):
             out=w_codes[:].bitcast(I32),
             in_=w_words.rearrange("k p d t -> p k (d t)").bitcast(I32),
         )
-        load_x(2)
         load_x(3)
         load_x(4)
 
@@ -95,7 +95,7 @@ def tile_clusternorm1dv3_e_kernel(tc, x, mu_track, w_words, w_scales, out):
             n, pair = divmod(half, PAIRS)
             centred = centred_pool.tile([P, 2, P, PACK], BF16, name="centred", align_bytes=64)
             in_order = xt_banks[half][:].bitcast(BF16).rearrange("p t (b c) -> p c b t", c=2)
-            if pair == PAIRS - 1 and n < SCALAR_HELPS_TILES:
+            if pair == PAIRS - 1 and n == SCALAR_HELPS_TILE:
                 ordered = ordered_pool.tile([P, 2, P, PACK], BF16, name="ordered")
                 nc.scalar.copy(out=ordered[:], in_=in_order)
                 in_order = ordered[:]
@@ -156,9 +156,9 @@ def tile_clusternorm1dv3_e_kernel(tc, x, mu_track, w_words, w_scales, out):
         transpose_tile(1)
         prepare_tile(0)
         for n in range(BATCH_TILES):
-            multiply_tile(n)
             if n + 2 < BATCH_TILES:
                 transpose_tile(n + 2)
+            multiply_tile(n)
             if n + 1 < BATCH_TILES:
                 prepare_tile(n + 1)
             copy_out_and_store(n)

@@ -20,7 +20,7 @@ D_TILES = FEATURES // D_TILE
 ROW = FEATURES * CLUSTERS
 WORDS_PER_P = ROW // 2 // P
 QUADRANTS = 4
-SCALAR_HELPS_TILE = 1
+SCALAR_HELPS_TILES = 2
 
 FLOPS = 2 * BATCH * FEATURES * FEATURES * CLUSTERS
 
@@ -32,7 +32,7 @@ def tile_clusternorm1dv3_e_kernel(tc, x, mu_track, w_words, w_scales, out):
 
     with ExitStack() as ctx:
         keep = ctx.enter_context(tc.tile_pool(name="keep", bufs=1))
-        ordered_pool = ctx.enter_context(tc.tile_pool(name="ordered_pool", bufs=1))
+        ordered_pool = ctx.enter_context(tc.tile_pool(name="ordered_pool", bufs=2))
         centred_pool = ctx.enter_context(tc.tile_pool(name="centred_pool", bufs=4))
         result_pool = ctx.enter_context(tc.tile_pool(name="result_pool", bufs=8))
         xt_pool = ctx.enter_context(tc.psum_pool(name="xt_pool", bufs=2 * PAIRS))
@@ -40,7 +40,8 @@ def tile_clusternorm1dv3_e_kernel(tc, x, mu_track, w_words, w_scales, out):
         ctx.enter_context(tc.manual_schedule())
 
         identity = keep.tile([P, P], F32)
-        mu_sb = keep.tile([P, PACK * CLUSTERS], BF16)
+        mu_loaded = keep.tile([P, PACK, CLUSTERS], BF16)
+        mu_sb = keep.tile([P, CLUSTERS, PACK], BF16)
         w_codes = keep.tile([P, CLUSTERS, FEATURES], U32, align_bytes=64)
         w_planes = keep.tile([P, FEATURES], U8, align_bytes=64)
         x_sb = [keep.tile([P, ROW], BF16, name="x_sb%d" % n) for n in range(BATCH_TILES)]
@@ -59,10 +60,9 @@ def tile_clusternorm1dv3_e_kernel(tc, x, mu_track, w_words, w_scales, out):
         def load_x(n):
             nc.sync.dma_start(out=x_sb[n][:], in_=x_rows[n])
 
-        nc.sync.dma_start(out=mu_sb[:], in_=mu_track.rearrange("(p t) k -> p (t k)", t=PACK))
+        nc.sync.dma_start(out=mu_loaded[:], in_=mu_track.rearrange("(p t) k -> p t k", t=PACK))
         load_x(0)
         load_x(1)
-        load_x(2)
         for quadrant in range(QUADRANTS):
             nc.sync.dma_start(
                 out=w_planes[32 * quadrant : 32 * quadrant + 4 * CLUSTERS, :].bitcast(I32),
@@ -72,8 +72,11 @@ def tile_clusternorm1dv3_e_kernel(tc, x, mu_track, w_words, w_scales, out):
             out=w_codes[:].bitcast(I32),
             in_=w_words.rearrange("k p d t -> p k (d t)").bitcast(I32),
         )
+        load_x(2)
         load_x(3)
         load_x(4)
+
+        nc.vector.tensor_copy(out=mu_sb[:], in_=mu_loaded[:].rearrange("p t k -> p k t"))
 
         xt_banks = {}
         centred_tiles = {}
@@ -95,11 +98,11 @@ def tile_clusternorm1dv3_e_kernel(tc, x, mu_track, w_words, w_scales, out):
             n, pair = divmod(half, PAIRS)
             centred = centred_pool.tile([P, 2, P, PACK], BF16, name="centred", align_bytes=64)
             in_order = xt_banks[half][:].bitcast(BF16).rearrange("p t (b c) -> p c b t", c=2)
-            if pair == PAIRS - 1 and n == SCALAR_HELPS_TILE:
+            if pair == PAIRS - 1 and n < SCALAR_HELPS_TILES:
                 ordered = ordered_pool.tile([P, 2, P, PACK], BF16, name="ordered")
                 nc.scalar.copy(out=ordered[:], in_=in_order)
                 in_order = ordered[:]
-            mu_of_pair = mu_sb[:].rearrange("p (t k) -> p k t", k=CLUSTERS)[:, 2 * pair : 2 * pair + 2, :]
+            mu_of_pair = mu_sb[:, 2 * pair : 2 * pair + 2, :]
             nc.vector.tensor_tensor(
                 out=centred[:],
                 in0=in_order,
@@ -156,9 +159,9 @@ def tile_clusternorm1dv3_e_kernel(tc, x, mu_track, w_words, w_scales, out):
         transpose_tile(1)
         prepare_tile(0)
         for n in range(BATCH_TILES):
+            multiply_tile(n)
             if n + 2 < BATCH_TILES:
                 transpose_tile(n + 2)
-            multiply_tile(n)
             if n + 1 < BATCH_TILES:
                 prepare_tile(n + 1)
             copy_out_and_store(n)

@@ -20,7 +20,7 @@ D_TILES = FEATURES // D_TILE
 ROW = FEATURES * CLUSTERS
 WORDS_PER_P = ROW // 2 // P
 QUADRANTS = 4
-SCALAR_HELPS_TILES = 2
+SCALAR_TAKES_PAIR_OF_TILE = 1
 
 FLOPS = 2 * BATCH * FEATURES * FEATURES * CLUSTERS
 
@@ -97,19 +97,27 @@ def tile_clusternorm1dv3_e_kernel(tc, x, mu_track, w_words, w_scales, out):
         def centre(half):
             n, pair = divmod(half, PAIRS)
             centred = centred_pool.tile([P, 2, P, PACK], BF16, name="centred", align_bytes=64)
-            in_order = xt_banks[half][:].bitcast(BF16).rearrange("p t (b c) -> p c b t", c=2)
-            if pair == PAIRS - 1 and n < SCALAR_HELPS_TILES:
-                ordered = ordered_pool.tile([P, 2, P, PACK], BF16, name="ordered")
-                nc.scalar.copy(out=ordered[:], in_=in_order)
-                in_order = ordered[:]
-            mu_of_pair = mu_sb[:, 2 * pair : 2 * pair + 2, :]
-            nc.vector.tensor_tensor(
-                out=centred[:],
-                in0=in_order,
-                in1=mu_of_pair.unsqueeze(2).to_broadcast([P, 2, P, PACK]),
-                op=mybir.AluOpType.subtract,
-            )
             centred_tiles[half] = centred
+            in_order = xt_banks[half][:].bitcast(BF16).rearrange("p t (b c) -> p c b t", c=2)
+
+            def subtract_mu(source, first, count):
+                mu = mu_sb[:, 2 * pair + first : 2 * pair + first + count, :]
+                nc.vector.tensor_tensor(
+                    out=centred[:, first : first + count],
+                    in0=source,
+                    in1=mu.unsqueeze(2).to_broadcast([P, count, P, PACK]),
+                    op=mybir.AluOpType.subtract,
+                )
+
+            if pair == 0:
+                subtract_mu(in_order, 0, 2)
+                return
+            first = 0 if n == SCALAR_TAKES_PAIR_OF_TILE else 1
+            ordered = ordered_pool.tile([P, 2, P, PACK], BF16, name="ordered")
+            nc.scalar.copy(out=ordered[:, first:2], in_=in_order[:, first:2])
+            if first == 1:
+                subtract_mu(in_order[:, 0:1], 0, 1)
+            subtract_mu(ordered[:, first:2], first, 2 - first)
 
         def quantise(half):
             n, pair = divmod(half, PAIRS)

@@ -22,6 +22,8 @@ WORDS_PER_P = ROW // 2 // P
 QUADRANTS = 4
 SCALAR_TAKES_PAIR_OF_TILE = 1
 
+WARM_UP_MATMULS = 4
+
 FLOPS = 2 * BATCH * FEATURES * FEATURES * CLUSTERS
 
 
@@ -40,6 +42,7 @@ def tile_clusternorm1dv3_e_kernel(tc, x, mu_track, w_words, w_scales, out):
         ctx.enter_context(tc.manual_schedule())
 
         identity = keep.tile([P, P], F32)
+        ones = keep.tile([P, D_TILE * CLUSTERS], BF16)
         mu_loaded = keep.tile([P, PACK, CLUSTERS], BF16)
         mu_sb = keep.tile([P, CLUSTERS, PACK], BF16)
         w_codes = keep.tile([P, CLUSTERS, FEATURES], U32, align_bytes=64)
@@ -54,13 +57,14 @@ def tile_clusternorm1dv3_e_kernel(tc, x, mu_track, w_words, w_scales, out):
             for n in range(BATCH_TILES)
         ]
 
+        nc.vector.memset(ones[:], 1.0)
         nc.vector.memset(w_planes[:].bitcast(I32), 0)
         make_identity(nc, identity[:])
 
         def load_x(n):
             nc.sync.dma_start(out=x_sb[n][:], in_=x_rows[n])
 
-        nc.sync.dma_start(out=mu_loaded[:], in_=mu_track.rearrange("(p t) k -> p t k", t=PACK))
+        nc.scalar.dma_start(out=mu_loaded[:], in_=mu_track.rearrange("(p t) k -> p t k", t=PACK))
         load_x(0)
         load_x(1)
         for quadrant in range(QUADRANTS):
@@ -81,6 +85,13 @@ def tile_clusternorm1dv3_e_kernel(tc, x, mu_track, w_words, w_scales, out):
         xt_banks = {}
         centred_tiles = {}
         product_banks = {}
+
+        def warm_up():
+            unread = product_pool.tile([P, CLUSTERS, D_TILE], F32, name="product")
+            for turn in range(WARM_UP_MATMULS):
+                nc.tensor.matmul(
+                    unread[:].rearrange("b k d -> b (k d)"), ones[:, 0:P], ones[:], start=True, stop=True
+                )
 
         def transpose_tile(n):
             words = x_sb[n][:].bitcast(F32)
@@ -163,6 +174,7 @@ def tile_clusternorm1dv3_e_kernel(tc, x, mu_track, w_words, w_scales, out):
                     in_=result[:].rearrange("b d k -> b (d k)"),
                 )
 
+        warm_up()
         transpose_tile(0)
         transpose_tile(1)
         prepare_tile(0)

@@ -23,6 +23,7 @@ QUADRANTS = 4
 SCALAR_TAKES_PAIR_OF_TILE = 1
 
 WARM_UP_MATMULS = 4
+FILLERS_AFTER_TILE = (2, 3)
 
 FLOPS = 2 * BATCH * FEATURES * FEATURES * CLUSTERS
 
@@ -42,7 +43,7 @@ def tile_clusternorm1dv3_e_kernel(tc, x, mu_track, w_words, w_scales, out):
         ctx.enter_context(tc.manual_schedule())
 
         identity = keep.tile([P, P], F32)
-        ones = keep.tile([P, D_TILE * CLUSTERS], BF16)
+        ones = keep.tile([P, P], F32)
         mu_loaded = keep.tile([P, PACK, CLUSTERS], BF16)
         mu_sb = keep.tile([P, CLUSTERS, PACK], BF16)
         w_codes = keep.tile([P, CLUSTERS, FEATURES], U32, align_bytes=64)
@@ -86,12 +87,11 @@ def tile_clusternorm1dv3_e_kernel(tc, x, mu_track, w_words, w_scales, out):
         centred_tiles = {}
         product_banks = {}
 
-        def warm_up():
-            unread = product_pool.tile([P, CLUSTERS, D_TILE], F32, name="product")
-            for turn in range(WARM_UP_MATMULS):
-                nc.tensor.matmul(
-                    unread[:].rearrange("b k d -> b (k d)"), ones[:, 0:P], ones[:], start=True, stop=True
-                )
+        unread = product_pool.tile([P, CLUSTERS, D_TILE], F32, name="product")
+
+        def warm_up(matmuls):
+            for turn in range(matmuls):
+                nc.tensor.matmul(unread[:, 0, :], ones[:], ones[:], start=True, stop=True)
 
         def transpose_tile(n):
             words = x_sb[n][:].bitcast(F32)
@@ -174,9 +174,10 @@ def tile_clusternorm1dv3_e_kernel(tc, x, mu_track, w_words, w_scales, out):
                     in_=result[:].rearrange("b d k -> b (d k)"),
                 )
 
-        warm_up()
-        transpose_tile(0)
-        transpose_tile(1)
+        warm_up(WARM_UP_MATMULS)
+        for n in range(2):
+            transpose_tile(n)
+            warm_up(FILLERS_AFTER_TILE[n])
         prepare_tile(0)
         for n in range(BATCH_TILES):
             multiply_tile(n)

@@ -19,19 +19,21 @@ D_TILE = 128
 D_TILES = FEATURES // D_TILE
 ROW = FEATURES * CLUSTERS
 WORDS_PER_P = ROW // 2 // P
+BANKS_IN_A_STORE = (1, 1, 1, 1, 2)
 QUADRANTS = 4
-SCALAR_TAKES_PAIR_OF_TILE = 1
+SCALAR_REORDERS = (2, 2, 0, 1, 1)
+VECTOR_EMPTIES = {3: (3,), 4: (1, 3)}
 
 WARM_UP_MATMULS = 4
-FILLERS_AFTER_TILE = (2, 3)
+FILLERS_AFTER_TILE = (2, 1)
 
 FLOPS = 2 * BATCH * FEATURES * FEATURES * CLUSTERS
 
 
 def tile_clusternorm1dv3_e_kernel(tc, x, mu_track, w_words, w_scales, out):
     nc = tc.nc
-    x_rows = x.rearrange("(n b) e k -> n b (e k)", b=P)
-    out_rows = out.rearrange("(n b) d k -> n b (d k)", b=P)
+    x_rows = x.rearrange("(b n) e k -> b (n e k)", n=BATCH_TILES)
+    out_rows = out.rearrange("(b n) d k -> n b (d k)", n=BATCH_TILES)
 
     with ExitStack() as ctx:
         keep = ctx.enter_context(tc.tile_pool(name="keep", bufs=1))
@@ -48,7 +50,7 @@ def tile_clusternorm1dv3_e_kernel(tc, x, mu_track, w_words, w_scales, out):
         mu_sb = keep.tile([P, CLUSTERS, PACK], BF16)
         w_codes = keep.tile([P, CLUSTERS, FEATURES], U32, align_bytes=64)
         w_planes = keep.tile([P, FEATURES], U8, align_bytes=64)
-        x_sb = [keep.tile([P, ROW], BF16, name="x_sb%d" % n) for n in range(BATCH_TILES)]
+        x_sb = keep.tile([P, BATCH_TILES * ROW], BF16)
         x_codes = [
             keep.tile([P, CLUSTERS, P], U32, name="x_codes%d" % n, align_bytes=64)
             for n in range(BATCH_TILES)
@@ -62,8 +64,9 @@ def tile_clusternorm1dv3_e_kernel(tc, x, mu_track, w_words, w_scales, out):
         nc.vector.memset(w_planes[:].bitcast(I32), 0)
         make_identity(nc, identity[:])
 
-        def load_x(n):
-            nc.sync.dma_start(out=x_sb[n][:], in_=x_rows[n])
+        def load_x(first, tiles=1):
+            columns = slice(ROW * first, ROW * (first + tiles))
+            nc.sync.dma_start(out=x_sb[:, columns], in_=x_rows[:, columns])
 
         nc.scalar.dma_start(out=mu_loaded[:], in_=mu_track.rearrange("(p t) k -> p t k", t=PACK))
         load_x(0)
@@ -73,13 +76,14 @@ def tile_clusternorm1dv3_e_kernel(tc, x, mu_track, w_words, w_scales, out):
                 out=w_planes[32 * quadrant : 32 * quadrant + 4 * CLUSTERS, :].bitcast(I32),
                 in_=w_scales[:, 4 * quadrant : 4 * quadrant + 4, :].bitcast(I32),
             )
-        nc.sync.dma_start(
-            out=w_codes[:].bitcast(I32),
-            in_=w_words.rearrange("k p d t -> p k (d t)").bitcast(I32),
-        )
+        for pair in range(PAIRS):
+            clusters = slice(2 * pair, 2 * pair + 2)
+            nc.sync.dma_start(
+                out=w_codes[:, clusters, :].bitcast(I32),
+                in_=w_words[clusters].rearrange("k p d t -> p k (d t)").bitcast(I32),
+            )
         load_x(2)
-        load_x(3)
-        load_x(4)
+        load_x(3, 2)
 
         nc.vector.tensor_copy(out=mu_sb[:], in_=mu_loaded[:].rearrange("p t k -> p k t"))
 
@@ -94,7 +98,7 @@ def tile_clusternorm1dv3_e_kernel(tc, x, mu_track, w_words, w_scales, out):
                 nc.tensor.matmul(unread[:, 0, :], ones[:], ones[:], start=True, stop=True)
 
         def transpose_tile(n):
-            words = x_sb[n][:].bitcast(F32)
+            words = x_sb[:, ROW * n : ROW * (n + 1)].bitcast(F32)
             for pair in range(PAIRS):
                 xt = xt_pool.tile([P, PACK, P], F32, name="xt")
                 for t in range(PACK):
@@ -120,11 +124,19 @@ def tile_clusternorm1dv3_e_kernel(tc, x, mu_track, w_words, w_scales, out):
                     op=mybir.AluOpType.subtract,
                 )
 
-            if pair == 0:
+            if pair == 0 or SCALAR_REORDERS[n] == 0:
                 subtract_mu(in_order, 0, 2)
                 return
-            first = 0 if n == SCALAR_TAKES_PAIR_OF_TILE else 1
+            first = 2 - SCALAR_REORDERS[n]
             ordered = ordered_pool.tile([P, 2, P, PACK], BF16, name="ordered")
+            if n == 0:
+                for c in range(2):
+                    nc.scalar.copy(out=ordered[:, c : c + 1], in_=in_order[:, c : c + 1])
+                for c in range(2):
+                    subtract_mu(ordered[:, c : c + 1], c, 1)
+                    if c == 0:
+                        quantise(0)
+                return
             nc.scalar.copy(out=ordered[:, first:2], in_=in_order[:, first:2])
             if first == 1:
                 subtract_mu(in_order[:, 0:1], 0, 1)
@@ -142,37 +154,50 @@ def tile_clusternorm1dv3_e_kernel(tc, x, mu_track, w_words, w_scales, out):
         def prepare_tile(n):
             for pair in range(PAIRS):
                 centre(PAIRS * n + pair)
-            for pair in range(PAIRS):
+            for pair in range(1 if n == 0 else 0, PAIRS):
                 quantise(PAIRS * n + pair)
 
+        def multiply(n, j, clusters):
+            d_cols = slice(D_TILE * j, D_TILE * (j + 1))
+            for k in clusters:
+                nc.tensor.matmul_mx(
+                    out=product_banks[(n, j)][:, k, :],
+                    lhsT=x_codes[n][:, k, :].bitcast(FP8X4),
+                    lhsT_scale=x_planes[n][:, k, :],
+                    rhs=w_codes[:, k, d_cols].bitcast(FP8X4),
+                    rhs_scale=w_planes[4 * k : P, d_cols],
+                    start=True,
+                    stop=True,
+                )
+
         def multiply_tile(n):
-            for j in range(D_TILES):
-                product = product_pool.tile([P, CLUSTERS, D_TILE], F32, name="product")
-                d_cols = slice(D_TILE * j, D_TILE * (j + 1))
-                for k in range(CLUSTERS):
-                    nc.tensor.matmul_mx(
-                        out=product[:, k, :],
-                        lhsT=x_codes[n][:, k, :].bitcast(FP8X4),
-                        lhsT_scale=x_planes[n][:, k, :],
-                        rhs=w_codes[:, k, d_cols].bitcast(FP8X4),
-                        rhs_scale=w_planes[4 * k : P, d_cols],
-                        start=True,
-                        stop=True,
-                    )
-                product_banks[(n, j)] = product
+            for first in range(0, D_TILES, 2):
+                banks = range(first, first + 2)
+                for j in banks:
+                    product_banks[(n, j)] = product_pool.tile([P, CLUSTERS, D_TILE], F32, name="product")
+                if n in (0, BATCH_TILES - 1) and first == 0:
+                    for pair in range(PAIRS):
+                        for j in banks:
+                            multiply(n, j, range(2 * pair, 2 * pair + 2))
+                else:
+                    for j in banks:
+                        multiply(n, j, range(CLUSTERS))
 
         def copy_out_and_store(n):
+            banks = BANKS_IN_A_STORE[n]
             for j in range(D_TILES):
-                result = result_pool.tile([P, D_TILE, CLUSTERS], F32, name="result")
+                if j % banks == 0:
+                    result = result_pool.tile([P, banks, D_TILE, CLUSTERS], F32, name="result%d" % banks)
                 interleaved = product_banks[(n, j)][:].rearrange("b k d -> b d k")
-                if n == BATCH_TILES - 1 and j % 2 == 1:
-                    nc.vector.tensor_copy(out=result[:], in_=interleaved)
+                if j in VECTOR_EMPTIES.get(n, ()):
+                    nc.vector.tensor_copy(out=result[:, j % banks], in_=interleaved)
                 else:
-                    nc.scalar.copy(out=result[:], in_=interleaved)
-                nc.sync.dma_start(
-                    out=out_rows[n][:, D_TILE * CLUSTERS * j : D_TILE * CLUSTERS * (j + 1)],
-                    in_=result[:].rearrange("b d k -> b (d k)"),
-                )
+                    nc.scalar.copy(out=result[:, j % banks], in_=interleaved)
+                if j % banks == banks - 1:
+                    nc.sync.dma_start(
+                        out=out_rows[n][:, D_TILE * CLUSTERS * (j + 1 - banks) : D_TILE * CLUSTERS * (j + 1)],
+                        in_=result[:].rearrange("b j d k -> b (j d k)"),
+                    )
 
         warm_up(WARM_UP_MATMULS)
         for n in range(2):

@@ -19,7 +19,7 @@ D_TILE = 128
 D_TILES = FEATURES // D_TILE
 ROW = FEATURES * CLUSTERS
 WORDS_PER_P = ROW // 2 // P
-BANKS_IN_A_STORE = (1, 1, 1, 1, 2)
+BANKS_IN_A_STORE = (1, 2, 2, 2, 2)
 QUADRANTS = 4
 SCALAR_REORDERS = (2, 2, 0, 1, 1)
 VECTOR_EMPTIES = {3: (3,), 4: (1, 3)}

@@ -19,10 +19,10 @@ D_TILE = 128
 D_TILES = FEATURES // D_TILE
 ROW = FEATURES * CLUSTERS
 WORDS_PER_P = ROW // 2 // P
-BANKS_IN_A_STORE = (1, 2, 2, 2, 2)
+STORES = ((1, 1, 1, 1), (2, 2), (2, 2), (2, 2), (1, 1, 2))
 QUADRANTS = 4
 SCALAR_REORDERS = (2, 2, 0, 1, 1)
-VECTOR_EMPTIES = {3: (3,), 4: (1, 3)}
+VECTOR_EMPTIES = {4: (0, 2)}
 
 WARM_UP_MATMULS = 4
 FILLERS_AFTER_TILE = (2, 1)
@@ -184,20 +184,20 @@ def tile_clusternorm1dv3_e_kernel(tc, x, mu_track, w_words, w_scales, out):
                         multiply(n, j, range(CLUSTERS))
 
         def copy_out_and_store(n):
-            banks = BANKS_IN_A_STORE[n]
-            for j in range(D_TILES):
-                if j % banks == 0:
-                    result = result_pool.tile([P, banks, D_TILE, CLUSTERS], F32, name="result%d" % banks)
-                interleaved = product_banks[(n, j)][:].rearrange("b k d -> b d k")
-                if j in VECTOR_EMPTIES.get(n, ()):
-                    nc.vector.tensor_copy(out=result[:, j % banks], in_=interleaved)
-                else:
-                    nc.scalar.copy(out=result[:, j % banks], in_=interleaved)
-                if j % banks == banks - 1:
-                    nc.sync.dma_start(
-                        out=out_rows[n][:, D_TILE * CLUSTERS * (j + 1 - banks) : D_TILE * CLUSTERS * (j + 1)],
-                        in_=result[:].rearrange("b j d k -> b (j d k)"),
-                    )
+            first = 0
+            for banks in STORES[n]:
+                result = result_pool.tile([P, banks, D_TILE, CLUSTERS], F32, name="result%d" % banks)
+                for j in range(first, first + banks):
+                    interleaved = product_banks[(n, j)][:].rearrange("b k d -> b d k")
+                    if j in VECTOR_EMPTIES.get(n, ()):
+                        nc.vector.tensor_copy(out=result[:, j - first], in_=interleaved)
+                    else:
+                        nc.scalar.copy(out=result[:, j - first], in_=interleaved)
+                nc.sync.dma_start(
+                    out=out_rows[n][:, D_TILE * CLUSTERS * first : D_TILE * CLUSTERS * (first + banks)],
+                    in_=result[:].rearrange("b j d k -> b (j d k)"),
+                )
+                first += banks
 
         warm_up(WARM_UP_MATMULS)
         for n in range(2):

@@ -19,9 +19,9 @@ D_TILE = 128
 D_TILES = FEATURES // D_TILE
 ROW = FEATURES * CLUSTERS
 WORDS_PER_P = ROW // 2 // P
-STORES = ((1, 1, 1, 1), (2, 2), (2, 2), (2, 2), (1, 1, 2))
+STORES = ((1, 1, 2), (2, 2), (2, 2), (2, 2), (1, 1, 2))
 QUADRANTS = 4
-SCALAR_REORDERS = (2, 2, 0, 1, 1)
+SCALAR_REORDERS = (2, 2, 0, 1, 0)
 VECTOR_EMPTIES = {4: (0, 2)}
 
 WARM_UP_MATMULS = 4

from contextlib import ExitStack

import concourse.mybir as mybir
from concourse.masks import make_identity

F32 = mybir.dt.float32
BF16 = mybir.dt.bfloat16
I32 = mybir.dt.int32
U32 = mybir.dt.uint32
U8 = mybir.dt.uint8
FP8X4 = mybir.dt.float8_e4m3fn_x4

P = 128
PACK = 4
BATCH, FEATURES, CLUSTERS = 640, 512, 4
PAIRS = CLUSTERS // 2
BATCH_TILES = BATCH // P
D_TILE = 128
D_TILES = FEATURES // D_TILE
ROW = FEATURES * CLUSTERS
WORDS_PER_P = ROW // 2 // P
STORES = ((1, 1, 2), (2, 2), (2, 2), (2, 2), (1, 1, 2))
QUADRANTS = 4
SCALAR_REORDERS = (2, 2, 0, 1, 0)
VECTOR_EMPTIES = {4: (0, 2)}

WARM_UP_MATMULS = 4
FILLERS_AFTER_TILE = (2, 1)

FLOPS = 2 * BATCH * FEATURES * FEATURES * CLUSTERS


def tile_clusternorm1dv3_e_kernel(tc, x, mu_track, w_words, w_scales, out):
    nc = tc.nc
    x_rows = x.rearrange("(b n) e k -> b (n e k)", n=BATCH_TILES)
    out_rows = out.rearrange("(b n) d k -> n b (d k)", n=BATCH_TILES)

    with ExitStack() as ctx:
        keep = ctx.enter_context(tc.tile_pool(name="keep", bufs=1))
        ordered_pool = ctx.enter_context(tc.tile_pool(name="ordered_pool", bufs=2))
        centred_pool = ctx.enter_context(tc.tile_pool(name="centred_pool", bufs=4))
        result_pool = ctx.enter_context(tc.tile_pool(name="result_pool", bufs=8))
        xt_pool = ctx.enter_context(tc.psum_pool(name="xt_pool", bufs=2 * PAIRS))
        product_pool = ctx.enter_context(tc.psum_pool(name="product_pool", bufs=D_TILES))
        ctx.enter_context(tc.manual_schedule())

        identity = keep.tile([P, P], F32)
        ones = keep.tile([P, P], F32)
        mu_loaded = keep.tile([P, PACK, CLUSTERS], BF16)
        mu_sb = keep.tile([P, CLUSTERS, PACK], BF16)
        w_codes = keep.tile([P, CLUSTERS, FEATURES], U32, align_bytes=64)
        w_planes = keep.tile([P, FEATURES], U8, align_bytes=64)
        x_sb = keep.tile([P, BATCH_TILES * ROW], BF16)
        x_codes = [
            keep.tile([P, CLUSTERS, P], U32, name="x_codes%d" % n, align_bytes=64)
            for n in range(BATCH_TILES)
        ]
        x_planes = [
            keep.tile([P, CLUSTERS, P], U8, name="x_planes%d" % n, align_bytes=64)
            for n in range(BATCH_TILES)
        ]

        nc.vector.memset(ones[:], 1.0)
        nc.vector.memset(w_planes[:].bitcast(I32), 0)
        make_identity(nc, identity[:])

        def load_x(first, tiles=1):
            columns = slice(ROW * first, ROW * (first + tiles))
            nc.sync.dma_start(out=x_sb[:, columns], in_=x_rows[:, columns])

        nc.scalar.dma_start(out=mu_loaded[:], in_=mu_track.rearrange("(p t) k -> p t k", t=PACK))
        load_x(0)
        load_x(1)
        for quadrant in range(QUADRANTS):
            nc.sync.dma_start(
                out=w_planes[32 * quadrant : 32 * quadrant + 4 * CLUSTERS, :].bitcast(I32),
                in_=w_scales[:, 4 * quadrant : 4 * quadrant + 4, :].bitcast(I32),
            )
        for pair in range(PAIRS):
            clusters = slice(2 * pair, 2 * pair + 2)
            nc.sync.dma_start(
                out=w_codes[:, clusters, :].bitcast(I32),
                in_=w_words[clusters].rearrange("k p d t -> p k (d t)").bitcast(I32),
            )
        load_x(2)
        load_x(3, 2)

        nc.vector.tensor_copy(out=mu_sb[:], in_=mu_loaded[:].rearrange("p t k -> p k t"))

        xt_banks = {}
        centred_tiles = {}
        product_banks = {}

        unread = product_pool.tile([P, CLUSTERS, D_TILE], F32, name="product")

        def warm_up(matmuls):
            for turn in range(matmuls):
                nc.tensor.matmul(unread[:, 0, :], ones[:], ones[:], start=True, stop=True)

        def transpose_tile(n):
            words = x_sb[:, ROW * n : ROW * (n + 1)].bitcast(F32)
            for pair in range(PAIRS):
                xt = xt_pool.tile([P, PACK, P], F32, name="xt")
                for t in range(PACK):
                    nc.tensor.transpose(
                        xt[:, t, :],
                        words[:, PAIRS * t + pair : ROW // 2 : WORDS_PER_P],
                        identity[:],
                    )
                xt_banks[PAIRS * n + pair] = xt

        def centre(half):
            n, pair = divmod(half, PAIRS)
            centred = centred_pool.tile([P, 2, P, PACK], BF16, name="centred", align_bytes=64)
            centred_tiles[half] = centred
            in_order = xt_banks[half][:].bitcast(BF16).rearrange("p t (b c) -> p c b t", c=2)

            def subtract_mu(source, first, count):
                mu = mu_sb[:, 2 * pair + first : 2 * pair + first + count, :]
                nc.vector.tensor_tensor(
                    out=centred[:, first : first + count],
                    in0=source,
                    in1=mu.unsqueeze(2).to_broadcast([P, count, P, PACK]),
                    op=mybir.AluOpType.subtract,
                )

            if pair == 0 or SCALAR_REORDERS[n] == 0:
                subtract_mu(in_order, 0, 2)
                return
            first = 2 - SCALAR_REORDERS[n]
            ordered = ordered_pool.tile([P, 2, P, PACK], BF16, name="ordered")
            if n == 0:
                for c in range(2):
                    nc.scalar.copy(out=ordered[:, c : c + 1], in_=in_order[:, c : c + 1])
                for c in range(2):
                    subtract_mu(ordered[:, c : c + 1], c, 1)
                    if c == 0:
                        quantise(0)
                return
            nc.scalar.copy(out=ordered[:, first:2], in_=in_order[:, first:2])
            if first == 1:
                subtract_mu(in_order[:, 0:1], 0, 1)
            subtract_mu(ordered[:, first:2], first, 2 - first)

        def quantise(half):
            n, pair = divmod(half, PAIRS)
            clusters = slice(2 * pair, 2 * pair + 2)
            nc.vector.quantize_mx(
                out=x_codes[n][:, clusters, :].rearrange("p c b -> p (c b)").bitcast(FP8X4),
                scales=x_planes[n][:, clusters, :].rearrange("p c b -> p (c b)"),
                in_=centred_tiles[half][:].rearrange("p c b t -> p (c b t)"),
            )

        def prepare_tile(n):
            for pair in range(PAIRS):
                centre(PAIRS * n + pair)
            for pair in range(1 if n == 0 else 0, PAIRS):
                quantise(PAIRS * n + pair)

        def multiply(n, j, clusters):
            d_cols = slice(D_TILE * j, D_TILE * (j + 1))
            for k in clusters:
                nc.tensor.matmul_mx(
                    out=product_banks[(n, j)][:, k, :],
                    lhsT=x_codes[n][:, k, :].bitcast(FP8X4),
                    lhsT_scale=x_planes[n][:, k, :],
                    rhs=w_codes[:, k, d_cols].bitcast(FP8X4),
                    rhs_scale=w_planes[4 * k : P, d_cols],
                    start=True,
                    stop=True,
                )

        def multiply_tile(n):
            for first in range(0, D_TILES, 2):
                banks = range(first, first + 2)
                for j in banks:
                    product_banks[(n, j)] = product_pool.tile([P, CLUSTERS, D_TILE], F32, name="product")
                if n in (0, BATCH_TILES - 1) and first == 0:
                    for pair in range(PAIRS):
                        for j in banks:
                            multiply(n, j, range(2 * pair, 2 * pair + 2))
                else:
                    for j in banks:
                        multiply(n, j, range(CLUSTERS))

        def copy_out_and_store(n):
            first = 0
            for banks in STORES[n]:
                result = result_pool.tile([P, banks, D_TILE, CLUSTERS], F32, name="result%d" % banks)
                for j in range(first, first + banks):
                    interleaved = product_banks[(n, j)][:].rearrange("b k d -> b d k")
                    if j in VECTOR_EMPTIES.get(n, ()):
                        nc.vector.tensor_copy(out=result[:, j - first], in_=interleaved)
                    else:
                        nc.scalar.copy(out=result[:, j - first], in_=interleaved)
                nc.sync.dma_start(
                    out=out_rows[n][:, D_TILE * CLUSTERS * first : D_TILE * CLUSTERS * (first + banks)],
                    in_=result[:].rearrange("b j d k -> b (j d k)"),
                )
                first += banks

        warm_up(WARM_UP_MATMULS)
        for n in range(2):
            transpose_tile(n)
            warm_up(FILLERS_AFTER_TILE[n])
        prepare_tile(0)
        for n in range(BATCH_TILES):
            multiply_tile(n)
            if n + 2 < BATCH_TILES:
                transpose_tile(n + 2)
            if n + 1 < BATCH_TILES:
                prepare_tile(n + 1)
            copy_out_and_store(n)
